import numpy as np
import ml_dtypes


def mxq(x, axis, fmt="e4m3"):
    dtype, down = {"e4m3": (ml_dtypes.float8_e4m3fn, 7), "e5m2": (ml_dtypes.float8_e5m2, 14)}[fmt]
    v = np.moveaxis(np.asarray(x, np.float32).astype(ml_dtypes.bfloat16).astype(np.float64), axis, -1)
    blocks = v.reshape(v.shape[:-1] + (-1, 32))
    amax = np.abs(blocks).max(-1, keepdims=True)
    byte = np.maximum(np.where(amax > 0, np.frexp(amax)[1] - 1 + 127, 0) - down, 1)
    scale = np.exp2(byte - 127.0)
    codes = (blocks / scale).astype(np.float32).astype(dtype).astype(np.float64)
    return np.moveaxis((codes * scale).reshape(v.shape), -1, axis)


WIDE = False


def mx_kscale(k):
    if not WIDE:
        return np.ones(k)
    levels = np.array([10, -10, 5, -5, 0])
    if k % 512:
        return np.exp2(np.random.permutation(np.resize(levels, k // 32))).repeat(32)
    a = np.empty((k // 512, 16))
    for p in range(k // 512):
        a[p, :8] = np.random.permutation(np.resize(levels, 8))
        for g in range(8):
            far = levels[np.abs(levels - a[p, g]) >= 10]
            a[p, g + 8] = far[np.random.randint(len(far))]
    return np.exp2(a.ravel()).repeat(32)


BF16 = ml_dtypes.bfloat16


def bf(x):
    return np.asarray(x, np.float32).astype(BF16)


def f64(x):
    return np.asarray(x).astype(np.float64)


B, N, D, H, DH = 2, 512, 1024, 8, 128
E = H * DH
GAIN = np.sqrt(1.8 / DH)


def setup_inputs():
    t = mx_kscale(E)
    return {"q_rot": bf(np.random.standard_normal((B, H, N, DH)) * GAIN),
            "k_rot": bf(np.random.standard_normal((B, H, N, DH)) * GAIN),
            "v": bf(np.random.standard_normal((B, H, N, DH)) * t.reshape(H, 1, DH)),
            "w_out": bf(np.random.standard_normal((E, D)) * E ** -0.5 / t[:, None]),
            "b_out": bf(np.random.standard_normal(D) * 0.2)}


def reference(q_rot, k_rot, v, w_out, b_out):
    scores = f64(q_rot) @ f64(k_rot).transpose(0, 1, 3, 2) * np.sqrt(DH)
    e = np.exp(scores - scores.max(-1, keepdims=True))
    p = e / e.sum(-1, keepdims=True)
    gate = p.sum(axis=2)
    attn = f64(v) * gate[..., None]
    attn = attn.transpose(0, 2, 1, 3).reshape(B, N, E)
    return (mxq(attn, 2, "e4m3") @ mxq(f64(w_out), 0, "e4m3")) + f64(b_out)

@@ -1,0 +1,303 @@
+from contextlib import ExitStack
+import math
+
+import concourse.masks as masks
+import concourse.mybir as mybir
+
+BF16 = mybir.dt.bfloat16
+F32 = mybir.dt.float32
+U32 = mybir.dt.uint32
+U8 = mybir.dt.uint8
+FP8X4 = mybir.dt.float8_e4m3fn_x4
+ACT = mybir.ActivationFunctionType
+ALU = mybir.AluOpType
+AX = mybir.AxisListType
+
+P = 128
+BATCHES, HEADS_PER_BATCH, TOKENS, D_OUT = 2, 8, 512, 1024
+HEADS = BATCHES * HEADS_PER_BATCH
+CHUNKS = TOKENS // P
+ALL_CHUNKS = HEADS * CHUNKS
+PACK = 4
+GROUPS = HEADS // PACK
+PARTS = GROUPS // BATCHES
+N_MX = 512
+SCALE = math.sqrt(P)
+FLOPS = 2 * HEADS * TOKENS * TOKENS * (P + 1) + 2 * BATCHES * TOKENS * HEADS_PER_BATCH * P * D_OUT
+
+TRANSPOSE_QK = -5
+COPY_QK = -4
+RECIPROCAL = 6
+SCALE_GPSIMD = 6
+SCALE_VECTOR = 8
+GATE = (12, 13, 13, 14)
+REDUCE = 15
+WEIGH = 16
+GROUP_READY = CHUNKS * (PACK - 1) + WEIGH
+TRANSPOSE_A = 2
+COPY_A = 3
+QUANTISE_A = 8
+PROJECT = 10
+W_LATE_HEAD = 5
+W_QUANTISE = ((22, 26), (46, 50))
+
+
+def tile_attn_pb_kernel(tc, q_rot, k_rot, v, w_out, b_out, out):
+    nc = tc.nc
+    with ExitStack() as ctx:
+        const = ctx.enter_context(tc.tile_pool(name="const", bufs=1))
+        keep = ctx.enter_context(tc.tile_pool(name="keep", bufs=1))
+        qk_pool = ctx.enter_context(tc.tile_pool(name="qkt", bufs=4))
+        e_pool = ctx.enter_context(tc.tile_pool(name="e", bufs=5))
+        st_pool = ctx.enter_context(tc.tile_pool(name="stat", bufs=6))
+        a_pool = ctx.enter_context(tc.tile_pool(name="a", bufs=2))
+        o_pool = ctx.enter_context(tc.tile_pool(name="o", bufs=6))
+        ps_s = ctx.enter_context(tc.psum_pool(name="ps_s", bufs=4))
+        ps_t = ctx.enter_context(tc.psum_pool(name="ps_t", bufs=1))
+        ps_c = ctx.enter_context(tc.psum_pool(name="ps_c", bufs=1))
+        ps_x = ctx.enter_context(tc.psum_pool(name="ps_x", bufs=2))
+        ctx.enter_context(tc.manual_schedule())
+
+        q_view = q_rot.rearrange("b h (p c) d -> p (b h) (c d)", c=CHUNKS)
+        k_view = k_rot.rearrange("b h (p c) d -> p (b h) (c d)", c=CHUNKS)
+        v_view = v.rearrange("b h (p c) d -> p (b h) (c d)", c=CHUNKS)
+        w_view = w_out.rearrange("(r p t) n -> p r t n", r=PARTS, t=PACK)
+        q_sb, k_sb, v_sb = {}, {}, {}
+
+        def load(dst, view, first, count, label):
+            t_in = keep.tile([P, count, TOKENS], BF16, name="%s%d" % (label, first))
+            nc.sync.dma_start(out=t_in[:], in_=view[:, first:first + count, :])
+            for h in range(count):
+                dst[first + h] = t_in[:, h, :]
+
+        w_raw = [keep.tile([P, PACK, D_OUT], BF16, name="wraw%d" % r) for r in range(PARTS)]
+        bias_bc = keep.tile([P, D_OUT], BF16, name="bias_bc")
+        for h in range(2):
+            load(q_sb, q_view, h, 1, "q")
+            load(k_sb, k_view, h, 1, "k")
+        nc.sync.dma_start(out=w_raw[0][:], in_=w_view[:, 0])
+        load(v_sb, v_view, 0, 2, "v")
+        load(q_sb, q_view, 2, 2, "q")
+        load(k_sb, k_view, 2, 2, "k")
+        nc.sync.dma_start(out=w_raw[1][:], in_=w_view[:, 1])
+        load(v_sb, v_view, 2, 2, "v")
+        nc.sync.dma_start(out=bias_bc[:], in_=b_out.partition_broadcast(P))
+        for first in range(4, HEADS, 2):
+            load(q_sb, q_view, first, 2, "q")
+            load(k_sb, k_view, first, 2, "k")
+            load(v_sb, v_view, first, 2, "v")
+
+        ident = const.tile([P, P], BF16, name="ident")
+        masks.make_identity(nc, ident[:])
+        ident_f = const.tile([P, P], F32, name="ident_f")
+        masks.make_identity(nc, ident_f[:])
+        warm = const.tile([P, 2], F32, name="warm")
+        nc.vector.memset(warm[:], 0.0)
+        nc.scalar.activation(out=warm[:, 1:2], in_=warm[:, 0:1], func=ACT.Exp)
+
+        w_grouped = [keep.tile([P, D_OUT, PACK], BF16, name="wgrp%d" % r, align_bytes=64) for r in range(PARTS)]
+        w_codes = keep.tile([P, PARTS, D_OUT], U32, name="w_codes", align_bytes=64)
+        w_scales = keep.tile([P, PARTS, D_OUT], U8, name="w_scales", align_bytes=64)
+
+        def regroup_w(r, quarter):
+            cols = slice(quarter * D_OUT // 4, (quarter + 1) * D_OUT // 4)
+            nc.gpsimd.tensor_scalar(out=w_grouped[r][:, cols, :],
+                                    in0=w_raw[r][:, :, cols].rearrange("p t n -> p n t"),
+                                    scalar1=1.0, scalar2=0.0, op0=ALU.mult, op1=ALU.add)
+
+        def quantise_w(r, half):
+            cols = slice(half * N_MX, (half + 1) * N_MX)
+            nc.vector.quantize_mx(out=w_codes[:, r, cols].bitcast(FP8X4), scales=w_scales[:, r, cols],
+                                  in_=w_grouped[r][:, cols, :].rearrange("p n t -> p (n t)"))
+
+        qk_ps, qk_t, score, expo, gate_ps = {}, {}, {}, {}, {}
+        row_max, bias, row_sum, inv_sum, gate = {}, {}, {}, {}, {}
+
+        def transpose_qk(h):
+            qk_ps[h] = ps_t.tile([P, 2 * TOKENS], BF16, name="tp")
+            for half, src in enumerate((q_sb[h], k_sb[h])):
+                for c in range(CHUNKS):
+                    nc.tensor.transpose(out=qk_ps[h][:, half * TOKENS + c * P:half * TOKENS + (c + 1) * P],
+                                        in_=src[:, c * P:(c + 1) * P], identity=ident[:])
+
+        def copy_qk(h):
+            qk_t[h] = qk_pool.tile([P, 2 * TOKENS], BF16, name="qkT")
+            nc.scalar.copy(out=qk_t[h][:], in_=qk_ps[h][:])
+
+        def scores(s):
+            h, c = divmod(s, CHUNKS)
+            score[s] = ps_s.tile([P, TOKENS], F32, name="s_ps", tag="s")
+            nc.tensor.matmul(out=score[s][:], lhsT=qk_t[h][:, c * P:(c + 1) * P], rhs=qk_t[h][:, TOKENS:],
+                             start=True, stop=True)
+
+        def maximum(s):
+            h, c = divmod(s, CHUNKS)
+            if c == 0:
+                row_max[h] = st_pool.tile([P, CHUNKS], F32, name="mx")
+            nc.vector.tensor_reduce(out=row_max[h][:, c:c + 1], in_=score[s][:], axis=AX.X, op=ALU.max)
+
+        def exp_bias(s):
+            h, c = divmod(s, CHUNKS)
+            if c == 0:
+                bias[h] = st_pool.tile([P, CHUNKS], F32, name="nb")
+            nc.scalar.mul(out=bias[h][:, c:c + 1], in_=row_max[h][:, c:c + 1], mul=-SCALE)
+
+        def exponentials(s):
+            h, c = divmod(s, CHUNKS)
+            if c == 0:
+                row_sum[h] = st_pool.tile([P, CHUNKS], F32, name="rs")
+                expo[h] = e_pool.tile([P, CHUNKS, TOKENS], F32, name="e_t")
+            nc.scalar.activation(out=expo[h][:, c, :], in_=score[s][:], func=ACT.Exp,
+                                 bias=bias[h][:, c:c + 1], scale=SCALE, accum_out=row_sum[h][:, c:c + 1])
+
+        def reciprocal(h):
+            inv_sum[h] = st_pool.tile([P, CHUNKS], F32, name="rr")
+            nc.vector.reciprocal(out=inv_sum[h][:], in_=row_sum[h][:])
+
+        def scale_gpsimd(h, c):
+            nc.gpsimd.tensor_scalar(out=expo[h][:, c, :], in0=expo[h][:, c, :], scalar1=inv_sum[h][:, c:c + 1],
+                                    scalar2=0.0, op0=ALU.mult, op1=ALU.add)
+
+        def scale_vector(h, c):
+            nc.vector.tensor_scalar(out=expo[h][:, c, :], in0=expo[h][:, c, :], scalar1=inv_sum[h][:, c:c + 1],
+                                    scalar2=None, op0=ALU.mult)
+
+        def scale_scalar(h, c):
+            nc.scalar.activation(out=expo[h][:, c, :], in_=expo[h][:, c, :], func=ACT.Copy,
+                                 scale=inv_sum[h][:, c:c + 1])
+
+        def gate_sum(h, j):
+            if j == 0 and h < HEADS - 2:
+                gate_ps[h] = ps_c.tile([P, CHUNKS, P], F32, name="cg")
+            if j == 0 and h >= HEADS - 2:
+                gate_ps[h] = ps_s.tile([P, CHUNKS, P], F32, name="cg_s", tag="s")
+            for c in range(CHUNKS):
+                nc.tensor.matmul(out=gate_ps[h][:, j, :], lhsT=expo[h][:, c, j * P:(j + 1) * P], rhs=ident_f[:],
+                                 start=(c == 0), stop=(c == CHUNKS - 1), is_transpose=True)
+
+        def reduce_gate(h):
+            gate[h] = st_pool.tile([P, CHUNKS], F32, name="cv")
+            nc.vector.tensor_reduce(out=gate[h][:], in_=gate_ps[h][:], axis=AX.X, op=ALU.add)
+
+        weighed, a_ps, a_grouped, a_codes, a_scales = {}, {}, {}, {}, {}
+
+        def weigh(h):
+            g, t = divmod(h, PACK)
+            if t == 0:
+                weighed[g] = a_pool.tile([P, CHUNKS, 2, P, 2], BF16, name="a4")
+            for j in range(CHUNKS):
+                nc.vector.tensor_scalar(out=weighed[g][:, j, :, t * P // PACK:(t + 1) * P // PACK, :],
+                                        in0=v_sb[h][:, j * P:(j + 1) * P].rearrange("p (i u e) -> p u i e", u=2, e=2),
+                                        scalar1=gate[h][:, j:j + 1], scalar2=None, op0=ALU.mult)
+
+        def transpose_a(g):
+            words = weighed[g][:].rearrange("p j u w e -> p (j u w e)").bitcast(F32)
+            for pair in range(CHUNKS // 2):
+                a_ps[g, pair] = ps_x.tile([P, 2, 2, P], F32, name="ta_x", tag="x")
+            for j in range(CHUNKS):
+                for u in range(2):
+                    nc.tensor.transpose(out=a_ps[g, j // 2][:, j % 2, u, :],
+                                        in_=words[:, (2 * j + u) * P:(2 * j + u + 1) * P], identity=ident_f[:])
+
+        def copy_a(copy, g, j):
+            if j == 0:
+                a_grouped[g] = a_pool.tile([P, CHUNKS, P, PACK], BF16, name="grp", align_bytes=64)
+            cols = slice(j * 2 * P, (j + 1) * 2 * P)
+            copy(out=a_grouped[g][:].rearrange("p j x t -> p (j x t)").bitcast(F32)[:, cols],
+                 in_=a_ps[g, j // 2][:, j % 2, :, :].rearrange("p u x -> p x u"))
+
+        def quantise_a(g, pair):
+            if pair == 0:
+                a_codes[g] = keep.tile([P, TOKENS], U32, name="a_codes%d" % g, align_bytes=64)
+                a_scales[g] = keep.tile([P, TOKENS], U8, name="a_scales%d" % g, align_bytes=64)
+            cols = slice(pair * 2 * P, (pair + 1) * 2 * P)
+            nc.vector.quantize_mx(out=a_codes[g][:, cols].bitcast(FP8X4), scales=a_scales[g][:, cols],
+                                  in_=a_grouped[g][:, 2 * pair:2 * pair + 2].rearrange("p j x t -> p (j x t)"))
+
+        out_view = out.rearrange("b (p j) n -> b j p n", j=CHUNKS)
+
+        def project(b):
+            for j in range(CHUNKS):
+                for half in range(D_OUT // N_MX):
+                    cols = slice(half * N_MX, (half + 1) * N_MX)
+                    if b == BATCHES - 1:
+                        acc = ps_s.tile([P, N_MX], F32, name="o_s", tag="s")
+                    else:
+                        acc = ps_x.tile([P, N_MX], F32, name="o_x", tag="x")
+                    for r in range(PARTS):
+                        g = PARTS * b + r
+                        nc.tensor.matmul_mx(out=acc[:],
+                                            lhsT=a_codes[g][:, j * P:(j + 1) * P].bitcast(FP8X4),
+                                            lhsT_scale=a_scales[g][:, j * P:(j + 1) * P],
+                                            rhs=w_codes[:, r, cols].bitcast(FP8X4), rhs_scale=w_scales[:, r, cols],
+                                            start=(r == 0), stop=(r == PARTS - 1))
+                    o_sb = o_pool.tile([P, N_MX], F32, name="o_sb")
+                    nc.vector.tensor_tensor(out=o_sb[:], in0=acc[:], in1=bias_bc[:, cols], op=ALU.add)
+                    nc.sync.dma_start(out=out_view[b, j][:, cols], in_=o_sb[:])
+
+        def head_in(s, stage):
+            h, rest = divmod(s - stage, CHUNKS)
+            return h if rest == 0 and 0 <= h < HEADS else -1
+
+        def group_in(s, stage):
+            g, rest = divmod(s - GROUP_READY - stage, CHUNKS * PACK)
+            return g if rest == 0 and 0 <= g < GROUPS else -1
+
+        last = HEADS - 1
+        for quarter in range(4):
+            regroup_w(0, quarter)
+        for s in range(TRANSPOSE_QK, CHUNKS * PACK * (GROUPS - 1) + GROUP_READY + COPY_A + 1):
+            if 0 <= s + 1 < ALL_CHUNKS:
+                scores(s + 1)
+            if head_in(s, TRANSPOSE_QK) >= 0:
+                transpose_qk(head_in(s, TRANSPOSE_QK))
+            for j in range(CHUNKS):
+                if head_in(s, GATE[j]) >= 0:
+                    gate_sum(head_in(s, GATE[j]), j)
+            if group_in(s, TRANSPOSE_A) >= 0:
+                transpose_a(group_in(s, TRANSPOSE_A))
+            if 0 <= s < ALL_CHUNKS:
+                maximum(s)
+            if head_in(s, RECIPROCAL) >= 0:
+                reciprocal(head_in(s, RECIPROCAL))
+            if head_in(s, RECIPROCAL) == last:
+                scale_vector(last, 0)
+                scale_vector(last, 2)
+            if head_in(s, REDUCE) >= 0:
+                reduce_gate(head_in(s, REDUCE))
+            if head_in(s, WEIGH) >= 0:
+                weigh(head_in(s, WEIGH))
+            if 0 <= head_in(s, SCALE_VECTOR) < last:
+                scale_vector(head_in(s, SCALE_VECTOR), 3)
+            if 0 <= group_in(s, QUANTISE_A) < GROUPS - 1:
+                quantise_a(group_in(s, QUANTISE_A), 0)
+                quantise_a(group_in(s, QUANTISE_A), 1)
+            for r in range(PARTS):
+                for half in range(D_OUT // N_MX):
+                    if s == W_QUANTISE[r][half]:
+                        quantise_w(r, half)
+            if 0 <= s < ALL_CHUNKS:
+                exp_bias(s)
+            if 0 <= s - 1 < ALL_CHUNKS:
+                exponentials(s - 1)
+            if head_in(s, COPY_QK) >= 0:
+                copy_qk(head_in(s, COPY_QK))
+            if head_in(s, RECIPROCAL) == last:
+                scale_scalar(last, 1)
+                scale_scalar(last, 3)
+            for j in range(CHUNKS):
+                if 0 <= group_in(s, COPY_A + j) < GROUPS - 1:
+                    copy_a(nc.scalar.copy, group_in(s, COPY_A + j), j)
+            for c in range(3):
+                if 0 <= head_in(s, SCALE_GPSIMD + c) < last:
+                    scale_gpsimd(head_in(s, SCALE_GPSIMD + c), c)
+            if W_LATE_HEAD <= head_in(s, SCALE_GPSIMD + 3) < W_LATE_HEAD + 4:
+                regroup_w(1, head_in(s, SCALE_GPSIMD + 3) - W_LATE_HEAD)
+            if group_in(s, PROJECT) == PARTS - 1:
+                project(0)
+            if group_in(s, COPY_A) == GROUPS - 1:
+                for pair in range(CHUNKS // 2):
+                    copy_a(nc.scalar.copy, GROUPS - 1, 2 * pair)
+                    copy_a(nc.vector.tensor_copy, GROUPS - 1, 2 * pair + 1)
+                    quantise_a(GROUPS - 1, pair)
+                project(BATCHES - 1)

@@ -22,25 +22,26 @@ PACK = 4
 GROUPS = HEADS // PACK
 PARTS = GROUPS // BATCHES
 N_MX = 512
+HALVES = D_OUT // N_MX
+TILES = CHUNKS * HALVES
 SCALE = math.sqrt(P)
 FLOPS = 2 * HEADS * TOKENS * TOKENS * (P + 1) + 2 * BATCHES * TOKENS * HEADS_PER_BATCH * P * D_OUT
 
 TRANSPOSE_QK = -5
 COPY_QK = -4
+LEAD = 1
 RECIPROCAL = 6
-SCALE_GPSIMD = 6
-SCALE_VECTOR = 8
+RESCALE_VECTOR = 8
 GATE = (12, 13, 13, 14)
 REDUCE = 15
 WEIGH = 16
-GROUP_READY = CHUNKS * (PACK - 1) + WEIGH
-TRANSPOSE_A = 2
-COPY_A = 3
-QUANTISE_A = 8
-PROJECT = 10
-W_LATE_HEAD = 5
-W_QUANTISE = ((22, 26), (46, 50))
-
+TRANSPOSE_A = 1
+COPY_A = (2, 2, 3, 3)
+QUANTISE_A = 5
+PROJECT = (6, 8, 10, 12, 14, 16, 18, 19)
+W_PIECES = 16
+W_EARLY = 8
+W_QUANTISE = 3
 
 def tile_attn_pb_kernel(tc, q_rot, k_rot, v, w_out, b_out, out):
     nc = tc.nc
@@ -51,7 +52,7 @@ def tile_attn_pb_kernel(tc, q_rot, k_rot, v, w_out, b_out, out):
         e_pool = ctx.enter_context(tc.tile_pool(name="e", bufs=5))
         st_pool = ctx.enter_context(tc.tile_pool(name="stat", bufs=6))
         a_pool = ctx.enter_context(tc.tile_pool(name="a", bufs=2))
-        o_pool = ctx.enter_context(tc.tile_pool(name="o", bufs=6))
+        o_pool = ctx.enter_context(tc.tile_pool(name="o", bufs=8))
         ps_s = ctx.enter_context(tc.psum_pool(name="ps_s", bufs=4))
         ps_t = ctx.enter_context(tc.psum_pool(name="ps_t", bufs=1))
         ps_c = ctx.enter_context(tc.psum_pool(name="ps_c", bufs=1))
@@ -73,12 +74,13 @@ def tile_attn_pb_kernel(tc, q_rot, k_rot, v, w_out, b_out, out):
         w_raw = [keep.tile([P, PACK, D_OUT], BF16, name="wraw%d" % r) for r in range(PARTS)]
         bias_bc = keep.tile([P, D_OUT], BF16, name="bias_bc")
         for h in range(2):
-            load(q_sb, q_view, h, 1, "q")
             load(k_sb, k_view, h, 1, "k")
-        nc.sync.dma_start(out=w_raw[0][:], in_=w_view[:, 0])
-        load(v_sb, v_view, 0, 2, "v")
+            load(q_sb, q_view, h, 1, "q")
+            cols = slice(h * N_MX, (h + 1) * N_MX)
+            nc.sync.dma_start(out=w_raw[0][:, :, cols], in_=w_view[:, 0, :, cols])
         load(q_sb, q_view, 2, 2, "q")
         load(k_sb, k_view, 2, 2, "k")
+        load(v_sb, v_view, 0, 2, "v")
         nc.sync.dma_start(out=w_raw[1][:], in_=w_view[:, 1])
         load(v_sb, v_view, 2, 2, "v")
         nc.sync.dma_start(out=bias_bc[:], in_=b_out.partition_broadcast(P))
@@ -99,35 +101,44 @@ def tile_attn_pb_kernel(tc, q_rot, k_rot, v, w_out, b_out, out):
         w_codes = keep.tile([P, PARTS, D_OUT], U32, name="w_codes", align_bytes=64)
         w_scales = keep.tile([P, PARTS, D_OUT], U8, name="w_scales", align_bytes=64)
 
-        def regroup_w(r, quarter):
-            cols = slice(quarter * D_OUT // 4, (quarter + 1) * D_OUT // 4)
-            nc.gpsimd.tensor_scalar(out=w_grouped[r][:, cols, :],
-                                    in0=w_raw[r][:, :, cols].rearrange("p t n -> p n t"),
-                                    scalar1=1.0, scalar2=0.0, op0=ALU.mult, op1=ALU.add)
+        def regroup_w(engine, piece):
+            r, part = divmod(piece, W_PIECES // PARTS)
+            cols = slice(part * P, (part + 1) * P)
+            engine.tensor_scalar(out=w_grouped[r][:, cols, :],
+                                 in0=w_raw[r][:, :, cols].rearrange("p t n -> p n t"),
+                                 scalar1=1.0, scalar2=0.0, op0=ALU.mult, op1=ALU.add)
 
-        def quantise_w(r, half):
-            cols = slice(half * N_MX, (half + 1) * N_MX)
+        def quantise_w(r, quarter):
+            cols = slice(quarter * D_OUT // 4, (quarter + 1) * D_OUT // 4)
             nc.vector.quantize_mx(out=w_codes[:, r, cols].bitcast(FP8X4), scales=w_scales[:, r, cols],
                                   in_=w_grouped[r][:, cols, :].rearrange("p n t -> p (n t)"))
 
-        qk_ps, qk_t, score, expo, gate_ps = {}, {}, {}, {}, {}
+        qk_ps, qk_t, score, expo, gate_ps, gate_all = {}, {}, {}, {}, {}, {}
         row_max, bias, row_sum, inv_sum, gate = {}, {}, {}, {}, {}
 
         def transpose_qk(h):
-            qk_ps[h] = ps_t.tile([P, 2 * TOKENS], BF16, name="tp")
-            for half, src in enumerate((q_sb[h], k_sb[h])):
+            bank = ps_t.tile([P, 2, TOKENS], BF16, name="tp", tag="tp")
+            qk_ps[h] = (bank[:, 0, :], bank[:, 1, :], bank[:])
+            if h == 0:
+                first = ps_x.tile([P, TOKENS], BF16, name="tp_x", tag="x")
+                qk_ps[h] = (bank[:, 0, :], first[:])
+            for half, src in ((1, k_sb[h]), (0, q_sb[h])):
                 for c in range(CHUNKS):
-                    nc.tensor.transpose(out=qk_ps[h][:, half * TOKENS + c * P:half * TOKENS + (c + 1) * P],
+                    nc.tensor.transpose(out=qk_ps[h][half][:, c * P:(c + 1) * P],
                                         in_=src[:, c * P:(c + 1) * P], identity=ident[:])
 
         def copy_qk(h):
-            qk_t[h] = qk_pool.tile([P, 2 * TOKENS], BF16, name="qkT")
-            nc.scalar.copy(out=qk_t[h][:], in_=qk_ps[h][:])
+            qk_t[h] = qk_pool.tile([P, 2, TOKENS], BF16, name="qkT")
+            if h == 0:
+                nc.vector.tensor_copy(out=qk_t[h][:, 1, :], in_=qk_ps[h][1])
+                nc.scalar.copy(out=qk_t[h][:, 0, :], in_=qk_ps[h][0])
+            else:
+                nc.scalar.copy(out=qk_t[h][:], in_=qk_ps[h][2])
 
         def scores(s):
             h, c = divmod(s, CHUNKS)
             score[s] = ps_s.tile([P, TOKENS], F32, name="s_ps", tag="s")
-            nc.tensor.matmul(out=score[s][:], lhsT=qk_t[h][:, c * P:(c + 1) * P], rhs=qk_t[h][:, TOKENS:],
+            nc.tensor.matmul(out=score[s][:], lhsT=qk_t[h][:, 0, c * P:(c + 1) * P], rhs=qk_t[h][:, 1, :],
                              start=True, stop=True)
 
         def maximum(s):
@@ -150,54 +161,57 @@ def tile_attn_pb_kernel(tc, q_rot, k_rot, v, w_out, b_out, out):
             nc.scalar.activation(out=expo[h][:, c, :], in_=score[s][:], func=ACT.Exp,
                                  bias=bias[h][:, c:c + 1], scale=SCALE, accum_out=row_sum[h][:, c:c + 1])
 
-        def reciprocal(h):
-            inv_sum[h] = st_pool.tile([P, CHUNKS], F32, name="rr")
-            nc.vector.reciprocal(out=inv_sum[h][:], in_=row_sum[h][:])
+        def reciprocals(h, first, end):
+            if first == 0:
+                inv_sum[h] = st_pool.tile([P, CHUNKS], F32, name="rr")
+            nc.vector.reciprocal(out=inv_sum[h][:, first:end], in_=row_sum[h][:, first:end])
 
-        def scale_gpsimd(h, c):
+        def rescale_gpsimd(h, c):
             nc.gpsimd.tensor_scalar(out=expo[h][:, c, :], in0=expo[h][:, c, :], scalar1=inv_sum[h][:, c:c + 1],
                                     scalar2=0.0, op0=ALU.mult, op1=ALU.add)
 
-        def scale_vector(h, c):
+        def rescale_vector(h, c):
             nc.vector.tensor_scalar(out=expo[h][:, c, :], in0=expo[h][:, c, :], scalar1=inv_sum[h][:, c:c + 1],
                                     scalar2=None, op0=ALU.mult)
 
-        def scale_scalar(h, c):
+        def rescale_scalar(h, c):
             nc.scalar.activation(out=expo[h][:, c, :], in_=expo[h][:, c, :], func=ACT.Copy,
                                  scale=inv_sum[h][:, c:c + 1])
 
+        def gate_add(h, j, c, i):
+            nc.tensor.matmul(out=gate_ps[h, j], lhsT=expo[h][:, c, j * P:(j + 1) * P], rhs=ident_f[:],
+                             start=(i == 0), stop=(i == CHUNKS - 1), is_transpose=True)
+
         def gate_sum(h, j):
-            if j == 0 and h < HEADS - 2:
-                gate_ps[h] = ps_c.tile([P, CHUNKS, P], F32, name="cg")
-            if j == 0 and h >= HEADS - 2:
-                gate_ps[h] = ps_s.tile([P, CHUNKS, P], F32, name="cg_s", tag="s")
+            if j == 0:
+                bank = ps_c.tile([P, CHUNKS, P], F32, name="cg", tag="c")
+                gate_all[h] = bank[:]
+            gate_ps[h, j] = gate_all[h][:, j, :]
             for c in range(CHUNKS):
-                nc.tensor.matmul(out=gate_ps[h][:, j, :], lhsT=expo[h][:, c, j * P:(j + 1) * P], rhs=ident_f[:],
-                                 start=(c == 0), stop=(c == CHUNKS - 1), is_transpose=True)
+                gate_add(h, j, c, c)
 
         def reduce_gate(h):
             gate[h] = st_pool.tile([P, CHUNKS], F32, name="cv")
-            nc.vector.tensor_reduce(out=gate[h][:], in_=gate_ps[h][:], axis=AX.X, op=ALU.add)
+            nc.vector.tensor_reduce(out=gate[h][:], in_=gate_all[h], axis=AX.X, op=ALU.add)
 
         weighed, a_ps, a_grouped, a_codes, a_scales = {}, {}, {}, {}, {}
 
-        def weigh(h):
+        def weigh(h, j):
             g, t = divmod(h, PACK)
-            if t == 0:
+            if t == 0 and j == 0:
                 weighed[g] = a_pool.tile([P, CHUNKS, 2, P, 2], BF16, name="a4")
-            for j in range(CHUNKS):
-                nc.vector.tensor_scalar(out=weighed[g][:, j, :, t * P // PACK:(t + 1) * P // PACK, :],
-                                        in0=v_sb[h][:, j * P:(j + 1) * P].rearrange("p (i u e) -> p u i e", u=2, e=2),
-                                        scalar1=gate[h][:, j:j + 1], scalar2=None, op0=ALU.mult)
+            nc.vector.tensor_scalar(out=weighed[g][:, j, :, t * P // PACK:(t + 1) * P // PACK, :],
+                                    in0=v_sb[h][:, j * P:(j + 1) * P].rearrange("p (i u e) -> p u i e", u=2, e=2),
+                                    scalar1=gate[h][:, j:j + 1], scalar2=None, op0=ALU.mult)
 
-        def transpose_a(g):
+        def transpose_a(g, pair, pool, tag):
             words = weighed[g][:].rearrange("p j u w e -> p (j u w e)").bitcast(F32)
-            for pair in range(CHUNKS // 2):
-                a_ps[g, pair] = ps_x.tile([P, 2, 2, P], F32, name="ta_x", tag="x")
-            for j in range(CHUNKS):
+            a_ps[g, pair] = pool.tile([P, 2, 2, P], F32, name="ta_" + tag, tag=tag)
+            for i in range(2):
                 for u in range(2):
-                    nc.tensor.transpose(out=a_ps[g, j // 2][:, j % 2, u, :],
-                                        in_=words[:, (2 * j + u) * P:(2 * j + u + 1) * P], identity=ident_f[:])
+                    first = (2 * (2 * pair + i) + u) * P
+                    nc.tensor.transpose(out=a_ps[g, pair][:, i, u, :], in_=words[:, first:first + P],
+                                        identity=ident_f[:])
 
         def copy_a(copy, g, j):
             if j == 0:
@@ -206,98 +220,170 @@ def tile_attn_pb_kernel(tc, q_rot, k_rot, v, w_out, b_out, out):
             copy(out=a_grouped[g][:].rearrange("p j x t -> p (j x t)").bitcast(F32)[:, cols],
                  in_=a_ps[g, j // 2][:, j % 2, :, :].rearrange("p u x -> p x u"))
 
-        def quantise_a(g, pair):
-            if pair == 0:
+        def quantise_a(g, first, count):
+            if first == 0:
                 a_codes[g] = keep.tile([P, TOKENS], U32, name="a_codes%d" % g, align_bytes=64)
                 a_scales[g] = keep.tile([P, TOKENS], U8, name="a_scales%d" % g, align_bytes=64)
-            cols = slice(pair * 2 * P, (pair + 1) * 2 * P)
+            cols = slice(first * P, (first + count) * P)
             nc.vector.quantize_mx(out=a_codes[g][:, cols].bitcast(FP8X4), scales=a_scales[g][:, cols],
-                                  in_=a_grouped[g][:, 2 * pair:2 * pair + 2].rearrange("p j x t -> p (j x t)"))
+                                  in_=a_grouped[g][:, first:first + count].rearrange("p j x t -> p (j x t)"))
 
         out_view = out.rearrange("b (p j) n -> b j p n", j=CHUNKS)
 
-        def project(b):
-            for j in range(CHUNKS):
-                for half in range(D_OUT // N_MX):
-                    cols = slice(half * N_MX, (half + 1) * N_MX)
-                    if b == BATCHES - 1:
-                        acc = ps_s.tile([P, N_MX], F32, name="o_s", tag="s")
-                    else:
-                        acc = ps_x.tile([P, N_MX], F32, name="o_x", tag="x")
-                    for r in range(PARTS):
-                        g = PARTS * b + r
-                        nc.tensor.matmul_mx(out=acc[:],
-                                            lhsT=a_codes[g][:, j * P:(j + 1) * P].bitcast(FP8X4),
-                                            lhsT_scale=a_scales[g][:, j * P:(j + 1) * P],
-                                            rhs=w_codes[:, r, cols].bitcast(FP8X4), rhs_scale=w_scales[:, r, cols],
-                                            start=(r == 0), stop=(r == PARTS - 1))
-                    o_sb = o_pool.tile([P, N_MX], F32, name="o_sb")
-                    nc.vector.tensor_tensor(out=o_sb[:], in0=acc[:], in1=bias_bc[:, cols], op=ALU.add)
-                    nc.sync.dma_start(out=out_view[b, j][:, cols], in_=o_sb[:])
+        def mx_pass(acc, b, tile, r):
+            j, half = divmod(tile, HALVES)
+            g = PARTS * b + r
+            cols = slice(half * N_MX, (half + 1) * N_MX)
+            nc.tensor.matmul_mx(out=acc[:],
+                                lhsT=a_codes[g][:, j * P:(j + 1) * P].bitcast(FP8X4),
+                                lhsT_scale=a_scales[g][:, j * P:(j + 1) * P],
+                                rhs=w_codes[:, r, cols].bitcast(FP8X4), rhs_scale=w_scales[:, r, cols],
+                                start=(r == 0), stop=(r == PARTS - 1))
+
+        def emit(acc, b, tile, shared):
+            j, half = divmod(tile, HALVES)
+            cols = slice(half * N_MX, (half + 1) * N_MX)
+            o_sb = o_pool.tile([P, N_MX], F32, name="o_sb")
+            if shared:
+                nc.scalar.copy(out=o_sb[:], in_=acc[:])
+                nc.gpsimd.tensor_tensor(out=o_sb[:], in0=o_sb[:], in1=bias_bc[:, cols], op=ALU.add)
+            else:
+                nc.vector.tensor_tensor(out=o_sb[:], in0=acc[:], in1=bias_bc[:, cols], op=ALU.add)
+            nc.sync.dma_start(out=out_view[b, j][:, cols], in_=o_sb[:])
 
         def head_in(s, stage):
             h, rest = divmod(s - stage, CHUNKS)
             return h if rest == 0 and 0 <= h < HEADS else -1
 
         def group_in(s, stage):
-            g, rest = divmod(s - GROUP_READY - stage, CHUNKS * PACK)
+            g, rest = divmod(s - (CHUNKS * (PACK - 1) + WEIGH) - stage, CHUNKS * PACK)
             return g if rest == 0 and 0 <= g < GROUPS else -1
 
         last = HEADS - 1
-        for quarter in range(4):
-            regroup_w(0, quarter)
-        for s in range(TRANSPOSE_QK, CHUNKS * PACK * (GROUPS - 1) + GROUP_READY + COPY_A + 1):
-            if 0 <= s + 1 < ALL_CHUNKS:
-                scores(s + 1)
+        acc = {}
+        for piece in range(W_EARLY):
+            regroup_w(nc.gpsimd, piece)
+        for s in range(TRANSPOSE_QK, ALL_CHUNKS):
+            if 0 <= s + LEAD < ALL_CHUNKS:
+                scores(s + LEAD)
             if head_in(s, TRANSPOSE_QK) >= 0:
                 transpose_qk(head_in(s, TRANSPOSE_QK))
             for j in range(CHUNKS):
-                if head_in(s, GATE[j]) >= 0:
+                if 0 <= head_in(s, GATE[j]) < last - 2:
                     gate_sum(head_in(s, GATE[j]), j)
-            if group_in(s, TRANSPOSE_A) >= 0:
-                transpose_a(group_in(s, TRANSPOSE_A))
+            if 0 <= group_in(s, TRANSPOSE_A) < GROUPS - 2:
+                for pair in range(2):
+                    transpose_a(group_in(s, TRANSPOSE_A), pair, ps_x, "x")
+            for tile in range(TILES):
+                if group_in(s, PROJECT[tile]) == PARTS - 1:
+                    acc[tile] = ps_x.tile([P, N_MX], F32, name="o_x", tag="x")
+                    for r in range(PARTS):
+                        mx_pass(acc[tile], 0, tile, r)
             if 0 <= s < ALL_CHUNKS:
                 maximum(s)
-            if head_in(s, RECIPROCAL) >= 0:
-                reciprocal(head_in(s, RECIPROCAL))
-            if head_in(s, RECIPROCAL) == last:
-                scale_vector(last, 0)
-                scale_vector(last, 2)
-            if head_in(s, REDUCE) >= 0:
+            if 0 <= head_in(s, RECIPROCAL) < last:
+                reciprocals(head_in(s, RECIPROCAL), 0, CHUNKS)
+            if 0 <= head_in(s, REDUCE) < last - 2:
                 reduce_gate(head_in(s, REDUCE))
-            if head_in(s, WEIGH) >= 0:
-                weigh(head_in(s, WEIGH))
-            if 0 <= head_in(s, SCALE_VECTOR) < last:
-                scale_vector(head_in(s, SCALE_VECTOR), 3)
+            if 0 <= head_in(s, WEIGH) < last - 2:
+                for j in range(CHUNKS):
+                    weigh(head_in(s, WEIGH), j)
+            if 0 <= head_in(s, RESCALE_VECTOR) < last - 1:
+                rescale_vector(head_in(s, RESCALE_VECTOR), 3)
             if 0 <= group_in(s, QUANTISE_A) < GROUPS - 1:
-                quantise_a(group_in(s, QUANTISE_A), 0)
-                quantise_a(group_in(s, QUANTISE_A), 1)
-            for r in range(PARTS):
-                for half in range(D_OUT // N_MX):
-                    if s == W_QUANTISE[r][half]:
-                        quantise_w(r, half)
+                for pair in range(2):
+                    quantise_a(group_in(s, QUANTISE_A), 2 * pair, 2)
+            if 0 <= head_in(s, RECIPROCAL + 1) - W_QUANTISE < 8:
+                quantise_w(*divmod(head_in(s, RECIPROCAL + 1) - W_QUANTISE, 4))
+            for tile in range(TILES):
+                if group_in(s, PROJECT[tile] + 1) == PARTS - 1:
+                    emit(acc[tile], 0, tile, False)
             if 0 <= s < ALL_CHUNKS:
                 exp_bias(s)
-            if 0 <= s - 1 < ALL_CHUNKS:
+            if 0 <= s - 1:
                 exponentials(s - 1)
             if head_in(s, COPY_QK) >= 0:
                 copy_qk(head_in(s, COPY_QK))
-            if head_in(s, RECIPROCAL) == last:
-                scale_scalar(last, 1)
-                scale_scalar(last, 3)
             for j in range(CHUNKS):
-                if 0 <= group_in(s, COPY_A + j) < GROUPS - 1:
-                    copy_a(nc.scalar.copy, group_in(s, COPY_A + j), j)
-            for c in range(3):
-                if 0 <= head_in(s, SCALE_GPSIMD + c) < last:
-                    scale_gpsimd(head_in(s, SCALE_GPSIMD + c), c)
-            if W_LATE_HEAD <= head_in(s, SCALE_GPSIMD + 3) < W_LATE_HEAD + 4:
-                regroup_w(1, head_in(s, SCALE_GPSIMD + 3) - W_LATE_HEAD)
-            if group_in(s, PROJECT) == PARTS - 1:
-                project(0)
-            if group_in(s, COPY_A) == GROUPS - 1:
-                for pair in range(CHUNKS // 2):
-                    copy_a(nc.scalar.copy, GROUPS - 1, 2 * pair)
-                    copy_a(nc.vector.tensor_copy, GROUPS - 1, 2 * pair + 1)
-                    quantise_a(GROUPS - 1, pair)
-                project(BATCHES - 1)
+                if 0 <= group_in(s, COPY_A[j]) < GROUPS - 2:
+                    copy_a(nc.scalar.copy, group_in(s, COPY_A[j]), j)
+            if 0 <= head_in(s, RECIPROCAL) < last:
+                for c in range(3):
+                    rescale_gpsimd(head_in(s, RECIPROCAL), c)
+                if W_EARLY + head_in(s, RECIPROCAL) < W_PIECES:
+                    regroup_w(nc.gpsimd, W_EARLY + head_in(s, RECIPROCAL))
+
+        def gate_banks(h, banks):
+            for j, (pool, tag) in enumerate(banks):
+                bank = pool.tile([P, P], F32, name="end_%d_%d" % (h, j), tag=tag)
+                gate_ps[h, j] = bank[:]
+
+        junk = const.tile([P, CHUNKS, P], BF16, name="junk")
+
+        def reduce_chunk(engine, h, j):
+            if j == 0:
+                gate[h] = st_pool.tile([P, CHUNKS], F32, name="cv")
+            if engine is nc.scalar:
+                nc.scalar.activation(out=junk[:, j, :], in_=gate_ps[h, j], func=ACT.Copy, accum_out=gate[h][:, j:j + 1])
+            else:
+                nc.vector.tensor_reduce(out=gate[h][:, j:j + 1], in_=gate_ps[h, j], axis=AX.X, op=ALU.add)
+
+        exponentials(ALL_CHUNKS - 1)
+        emit(acc[TILES - 1], 0, TILES - 1, False)
+        for j in range(CHUNKS):
+            weigh(last - 3, j)
+        rescale_vector(last - 1, 3)
+        reciprocals(last, 0, 3)
+        rescale_vector(last, 0)
+        rescale_vector(last, 1)
+        reciprocals(last, 3, 4)
+        rescale_vector(last, 2)
+        rescale_vector(last, 3)
+        bank = ps_t.tile([P, CHUNKS, P], F32, name="cg_t", tag="tp")
+        for j in range(CHUNKS):
+            gate_ps[last - 2, j] = bank[:, j, :]
+            for c in range(CHUNKS):
+                gate_add(last - 2, j, c, c)
+        for pair in range(2):
+            transpose_a(GROUPS - 2, pair, ps_x, "x")
+        bank = ps_c.tile([P, CHUNKS, P], F32, name="cg", tag="c")
+        for j in range(CHUNKS):
+            gate_ps[last - 1, j] = bank[:, j, :]
+            for c in range(CHUNKS):
+                gate_add(last - 1, j, c, c)
+        gate_banks(last, ((ps_s, "s"), (ps_s, "s"), (ps_s, "s"), (ps_s, "s")))
+        for c in range(CHUNKS):
+            for j in range(CHUNKS):
+                gate_add(last, j, c, c)
+        for j in range(CHUNKS):
+            reduce_chunk(nc.scalar, last - 2, j)
+        for j in range(CHUNKS):
+            copy_a(nc.scalar.copy, GROUPS - 2, j)
+        for j in range(CHUNKS):
+            weigh(last - 2, j)
+        for j in range(0, CHUNKS, 2):
+            quantise_a(GROUPS - 2, j, 2)
+        for j in range(CHUNKS):
+            reduce_chunk(nc.scalar, last - 1, j)
+        for j in range(CHUNKS):
+            reduce_chunk(nc.vector, last, j)
+        for j in range(CHUNKS):
+            weigh(last - 1, j)
+        for j in range(CHUNKS):
+            weigh(last, j)
+        banks = ((ps_x, "x"), (ps_x, "x"), (ps_t, "tp"), (ps_c, "c"))
+        for tile, (pool, tag) in enumerate(banks):
+            acc[tile] = pool.tile([P, N_MX], F32, name="o_e%d" % tile, tag=tag)
+            mx_pass(acc[tile], 1, tile, 0)
+        for pair in range(2):
+            transpose_a(GROUPS - 1, pair, ps_s, "s")
+        for j in range(CHUNKS):
+            copy_a((nc.scalar.copy, nc.vector.tensor_copy)[j // 2], GROUPS - 1, j)
+        for j in range(CHUNKS):
+            quantise_a(GROUPS - 1, j, 1)
+        for tile in range(TILES):
+            if tile >= len(banks):
+                acc[tile] = ps_s.tile([P, N_MX], F32, name="o_s", tag="s")
+                mx_pass(acc[tile], 1, tile, 0)
+            mx_pass(acc[tile], 1, tile, 1)
+            emit(acc[tile], 1, tile, False)

@@ -38,8 +38,9 @@ WEIGH = 16
 TRANSPOSE_A = 1
 COPY_A = (2, 2, 3, 3)
 QUANTISE_A = 5
-PROJECT = (6, 8, 10, 12, 14, 16, 18, 19)
+PROJECT = (6, 8, 9, 11, 12, 14, 15, 17)
 W_PIECES = 16
+MV_END = 12
 W_EARLY = 8
 W_QUANTISE = 3
 
@@ -133,7 +134,8 @@ def tile_attn_pb_kernel(tc, q_rot, k_rot, v, w_out, b_out, out):
                 nc.vector.tensor_copy(out=qk_t[h][:, 1, :], in_=qk_ps[h][1])
                 nc.scalar.copy(out=qk_t[h][:, 0, :], in_=qk_ps[h][0])
             else:
-                nc.scalar.copy(out=qk_t[h][:], in_=qk_ps[h][2])
+                nc.scalar.copy(out=qk_t[h][:].rearrange("p s n -> p (s n)").bitcast(F32),
+                               in_=qk_ps[h][2].rearrange("p s n -> p (s n)").bitcast(F32))
 
         def scores(s):
             h, c = divmod(s, CHUNKS)
@@ -179,12 +181,17 @@ def tile_attn_pb_kernel(tc, q_rot, k_rot, v, w_out, b_out, out):
                                  scale=inv_sum[h][:, c:c + 1])
 
         def gate_add(h, j, c, i):
-            nc.tensor.matmul(out=gate_ps[h, j], lhsT=expo[h][:, c, j * P:(j + 1) * P], rhs=ident_f[:],
-                             start=(i == 0), stop=(i == CHUNKS - 1), is_transpose=True)
+            block = expo[h][:, c, j * P:(j + 1) * P]
+            if c == CHUNKS - 1 and h < MV_END:
+                nc.tensor.matmul(out=gate_ps[h, j][:, 0:1], lhsT=block, rhs=inv_sum[h][:, c:c + 1],
+                                 start=(i == 0), stop=(i == CHUNKS - 1))
+            else:
+                nc.tensor.matmul(out=gate_ps[h, j], lhsT=block, rhs=ident_f[:],
+                                 start=(i == 0), stop=(i == CHUNKS - 1), is_transpose=True)
 
-        def gate_sum(h, j):
+        def gate_sum(h, j, pool=ps_c, tag="c"):
             if j == 0:
-                bank = ps_c.tile([P, CHUNKS, P], F32, name="cg", tag="c")
+                bank = pool.tile([P, CHUNKS, P], F32, name="cg_" + tag, tag=tag)
                 gate_all[h] = bank[:]
             gate_ps[h, j] = gate_all[h][:, j, :]
             for c in range(CHUNKS):
@@ -196,6 +203,14 @@ def tile_attn_pb_kernel(tc, q_rot, k_rot, v, w_out, b_out, out):
 
         weighed, a_ps, a_grouped, a_codes, a_scales = {}, {}, {}, {}, {}
 
+        def weigh_gpsimd(h, j):
+            g, t = divmod(h, PACK)
+            if t == 0 and j == 0:
+                weighed[g] = a_pool.tile([P, CHUNKS, 2, P, 2], BF16, name="a4")
+            nc.gpsimd.tensor_scalar(out=weighed[g][:, j, :, t * P // PACK:(t + 1) * P // PACK, :],
+                                    in0=v_sb[h][:, j * P:(j + 1) * P].rearrange("p (i u e) -> p u i e", u=2, e=2),
+                                    scalar1=gate[h][:, j:j + 1], scalar2=0.0, op0=ALU.mult, op1=ALU.add)
+
         def weigh(h, j):
             g, t = divmod(h, PACK)
             if t == 0 and j == 0:
@@ -204,21 +219,21 @@ def tile_attn_pb_kernel(tc, q_rot, k_rot, v, w_out, b_out, out):
                                     in0=v_sb[h][:, j * P:(j + 1) * P].rearrange("p (i u e) -> p u i e", u=2, e=2),
                                     scalar1=gate[h][:, j:j + 1], scalar2=None, op0=ALU.mult)
 
-        def transpose_a(g, pair, pool, tag):
+        def transpose_a(g, chunks, pool, tag):
             words = weighed[g][:].rearrange("p j u w e -> p (j u w e)").bitcast(F32)
-            a_ps[g, pair] = pool.tile([P, 2, 2, P], F32, name="ta_" + tag, tag=tag)
-            for i in range(2):
+            bank = pool.tile([P, len(chunks), 2, P], F32, name="ta_" + tag, tag=tag)
+            for i, j in enumerate(chunks):
+                a_ps[g, j] = bank[:, i]
                 for u in range(2):
-                    first = (2 * (2 * pair + i) + u) * P
-                    nc.tensor.transpose(out=a_ps[g, pair][:, i, u, :], in_=words[:, first:first + P],
-                                        identity=ident_f[:])
+                    first = (2 * j + u) * P
+                    nc.tensor.transpose(out=a_ps[g, j][:, u, :], in_=words[:, first:first + P], identity=ident_f[:])
 
         def copy_a(copy, g, j):
             if j == 0:
                 a_grouped[g] = a_pool.tile([P, CHUNKS, P, PACK], BF16, name="grp", align_bytes=64)
             cols = slice(j * 2 * P, (j + 1) * 2 * P)
             copy(out=a_grouped[g][:].rearrange("p j x t -> p (j x t)").bitcast(F32)[:, cols],
-                 in_=a_ps[g, j // 2][:, j % 2, :, :].rearrange("p u x -> p x u"))
+                 in_=a_ps[g, j].rearrange("p u x -> p x u"))
 
         def quantise_a(g, first, count):
             if first == 0:
@@ -273,24 +288,27 @@ def tile_attn_pb_kernel(tc, q_rot, k_rot, v, w_out, b_out, out):
                     gate_sum(head_in(s, GATE[j]), j)
             if 0 <= group_in(s, TRANSPOSE_A) < GROUPS - 2:
                 for pair in range(2):
-                    transpose_a(group_in(s, TRANSPOSE_A), pair, ps_x, "x")
+                    transpose_a(group_in(s, TRANSPOSE_A), (2 * pair, 2 * pair + 1), ps_x, "x")
             for tile in range(TILES):
                 if group_in(s, PROJECT[tile]) == PARTS - 1:
                     acc[tile] = ps_x.tile([P, N_MX], F32, name="o_x", tag="x")
                     for r in range(PARTS):
                         mx_pass(acc[tile], 0, tile, r)
-            if 0 <= s < ALL_CHUNKS:
-                maximum(s)
+            if s >= ALL_CHUNKS - 2:
+                for j in (2 * (s - ALL_CHUNKS) + 4, 2 * (s - ALL_CHUNKS) + 5):
+                    gate_sum(last - 2, j, ps_t, "tp")
             if 0 <= head_in(s, RECIPROCAL) < last:
                 reciprocals(head_in(s, RECIPROCAL), 0, CHUNKS)
+            if 0 <= s < ALL_CHUNKS:
+                maximum(s)
             if 0 <= head_in(s, REDUCE) < last - 2:
                 reduce_gate(head_in(s, REDUCE))
             if 0 <= head_in(s, WEIGH) < last - 2:
                 for j in range(CHUNKS):
                     weigh(head_in(s, WEIGH), j)
-            if 0 <= head_in(s, RESCALE_VECTOR) < last - 1:
+            if MV_END <= head_in(s, RESCALE_VECTOR) < last - 1:
                 rescale_vector(head_in(s, RESCALE_VECTOR), 3)
-            if 0 <= group_in(s, QUANTISE_A) < GROUPS - 1:
+            if 0 <= group_in(s, QUANTISE_A) < GROUPS - 2:
                 for pair in range(2):
                     quantise_a(group_in(s, QUANTISE_A), 2 * pair, 2)
             if 0 <= head_in(s, RECIPROCAL + 1) - W_QUANTISE < 8:
@@ -308,7 +326,7 @@ def tile_attn_pb_kernel(tc, q_rot, k_rot, v, w_out, b_out, out):
                 if 0 <= group_in(s, COPY_A[j]) < GROUPS - 2:
                     copy_a(nc.scalar.copy, group_in(s, COPY_A[j]), j)
             if 0 <= head_in(s, RECIPROCAL) < last:
-                for c in range(3):
+                for c in range(3 if head_in(s, RECIPROCAL) < last - 1 else 2):
                     rescale_gpsimd(head_in(s, RECIPROCAL), c)
                 if W_EARLY + head_in(s, RECIPROCAL) < W_PIECES:
                     regroup_w(nc.gpsimd, W_EARLY + head_in(s, RECIPROCAL))
@@ -329,61 +347,53 @@ def tile_attn_pb_kernel(tc, q_rot, k_rot, v, w_out, b_out, out):
                 nc.vector.tensor_reduce(out=gate[h][:, j:j + 1], in_=gate_ps[h, j], axis=AX.X, op=ALU.add)
 
         exponentials(ALL_CHUNKS - 1)
-        emit(acc[TILES - 1], 0, TILES - 1, False)
-        for j in range(CHUNKS):
-            weigh(last - 3, j)
+        for pair in range(2):
+            transpose_a(GROUPS - 2, (2 * pair, 2 * pair + 1), ps_x, "x")
+        rescale_vector(last - 1, 2)
         rescale_vector(last - 1, 3)
-        reciprocals(last, 0, 3)
+        reciprocals(last, 0, 2)
         rescale_vector(last, 0)
         rescale_vector(last, 1)
-        reciprocals(last, 3, 4)
+        for j in range(CHUNKS):
+            weigh_gpsimd(last - 3, j)
+        reciprocals(last, 2, 3)
         rescale_vector(last, 2)
+        reciprocals(last, 3, 4)
         rescale_vector(last, 3)
-        bank = ps_t.tile([P, CHUNKS, P], F32, name="cg_t", tag="tp")
         for j in range(CHUNKS):
-            gate_ps[last - 2, j] = bank[:, j, :]
-            for c in range(CHUNKS):
-                gate_add(last - 2, j, c, c)
-        for pair in range(2):
-            transpose_a(GROUPS - 2, pair, ps_x, "x")
-        bank = ps_c.tile([P, CHUNKS, P], F32, name="cg", tag="c")
-        for j in range(CHUNKS):
-            gate_ps[last - 1, j] = bank[:, j, :]
-            for c in range(CHUNKS):
-                gate_add(last - 1, j, c, c)
+            gate_sum(last - 1, j)
         gate_banks(last, ((ps_s, "s"), (ps_s, "s"), (ps_s, "s"), (ps_s, "s")))
         for c in range(CHUNKS):
             for j in range(CHUNKS):
                 gate_add(last, j, c, c)
         for j in range(CHUNKS):
-            reduce_chunk(nc.scalar, last - 2, j)
-        for j in range(CHUNKS):
             copy_a(nc.scalar.copy, GROUPS - 2, j)
-        for j in range(CHUNKS):
-            weigh(last - 2, j)
+        for h in (last - 2, last - 1):
+            for j in range(CHUNKS):
+                reduce_chunk(nc.scalar, h, j)
         for j in range(0, CHUNKS, 2):
             quantise_a(GROUPS - 2, j, 2)
         for j in range(CHUNKS):
-            reduce_chunk(nc.scalar, last - 1, j)
-        for j in range(CHUNKS):
-            reduce_chunk(nc.vector, last, j)
-        for j in range(CHUNKS):
-            weigh(last - 1, j)
-        for j in range(CHUNKS):
-            weigh(last, j)
+            weigh_gpsimd(last - 2, j)
         banks = ((ps_x, "x"), (ps_x, "x"), (ps_t, "tp"), (ps_c, "c"))
-        for tile, (pool, tag) in enumerate(banks):
+        for tile, (pool, tag) in enumerate(banks[:2]):
             acc[tile] = pool.tile([P, N_MX], F32, name="o_e%d" % tile, tag=tag)
             mx_pass(acc[tile], 1, tile, 0)
-        for pair in range(2):
-            transpose_a(GROUPS - 1, pair, ps_s, "s")
-        for j in range(CHUNKS):
-            copy_a((nc.scalar.copy, nc.vector.tensor_copy)[j // 2], GROUPS - 1, j)
-        for j in range(CHUNKS):
-            quantise_a(GROUPS - 1, j, 1)
+        for j in range(CHUNKS + 1):
+            if j < CHUNKS:
+                reduce_chunk(nc.vector, last, j)
+            if j > 0:
+                for h in (last - 1, last):
+                    weigh(h, j - 1)
+                transpose_a(GROUPS - 1, (j - 1,), ps_s, "s")
+                copy_a(nc.scalar.copy, GROUPS - 1, j - 1)
+        quantise_a(GROUPS - 1, 0, 1)
+        quantise_a(GROUPS - 1, 1, 1)
         for tile in range(TILES):
-            if tile >= len(banks):
+            if tile >= 2:
                 acc[tile] = ps_s.tile([P, N_MX], F32, name="o_s", tag="s")
                 mx_pass(acc[tile], 1, tile, 0)
+            if tile in (1, 3):
+                quantise_a(GROUPS - 1, tile // 2 + 2, 1)
             mx_pass(acc[tile], 1, tile, 1)
             emit(acc[tile], 1, tile, False)

from contextlib import ExitStack
import math

import concourse.masks as masks
import concourse.mybir as mybir

BF16 = mybir.dt.bfloat16
F32 = mybir.dt.float32
U32 = mybir.dt.uint32
U8 = mybir.dt.uint8
FP8X4 = mybir.dt.float8_e4m3fn_x4
ACT = mybir.ActivationFunctionType
ALU = mybir.AluOpType
AX = mybir.AxisListType

P = 128
BATCHES, HEADS_PER_BATCH, TOKENS, D_OUT = 2, 8, 512, 1024
HEADS = BATCHES * HEADS_PER_BATCH
CHUNKS = TOKENS // P
ALL_CHUNKS = HEADS * CHUNKS
PACK = 4
GROUPS = HEADS // PACK
PARTS = GROUPS // BATCHES
N_MX = 512
HALVES = D_OUT // N_MX
TILES = CHUNKS * HALVES
SCALE = math.sqrt(P)
FLOPS = 2 * HEADS * TOKENS * TOKENS * (P + 1) + 2 * BATCHES * TOKENS * HEADS_PER_BATCH * P * D_OUT

TRANSPOSE_QK = -5
COPY_QK = -4
LEAD = 1
RECIPROCAL = 6
RESCALE_VECTOR = 8
GATE = (12, 13, 13, 14)
REDUCE = 15
WEIGH = 16
TRANSPOSE_A = 1
COPY_A = (2, 2, 3, 3)
QUANTISE_A = 5
PROJECT = (6, 8, 9, 11, 12, 14, 15, 17)
W_PIECES = 16
MV_END = 12
W_EARLY = 8
W_QUANTISE = 3

def tile_attn_pb_kernel(tc, q_rot, k_rot, v, w_out, b_out, out):
    nc = tc.nc
    with ExitStack() as ctx:
        const = ctx.enter_context(tc.tile_pool(name="const", bufs=1))
        keep = ctx.enter_context(tc.tile_pool(name="keep", bufs=1))
        qk_pool = ctx.enter_context(tc.tile_pool(name="qkt", bufs=4))
        e_pool = ctx.enter_context(tc.tile_pool(name="e", bufs=5))
        st_pool = ctx.enter_context(tc.tile_pool(name="stat", bufs=6))
        a_pool = ctx.enter_context(tc.tile_pool(name="a", bufs=2))
        o_pool = ctx.enter_context(tc.tile_pool(name="o", bufs=8))
        ps_s = ctx.enter_context(tc.psum_pool(name="ps_s", bufs=4))
        ps_t = ctx.enter_context(tc.psum_pool(name="ps_t", bufs=1))
        ps_c = ctx.enter_context(tc.psum_pool(name="ps_c", bufs=1))
        ps_x = ctx.enter_context(tc.psum_pool(name="ps_x", bufs=2))
        ctx.enter_context(tc.manual_schedule())

        q_view = q_rot.rearrange("b h (p c) d -> p (b h) (c d)", c=CHUNKS)
        k_view = k_rot.rearrange("b h (p c) d -> p (b h) (c d)", c=CHUNKS)
        v_view = v.rearrange("b h (p c) d -> p (b h) (c d)", c=CHUNKS)
        w_view = w_out.rearrange("(r p t) n -> p r t n", r=PARTS, t=PACK)
        q_sb, k_sb, v_sb = {}, {}, {}

        def load(dst, view, first, count, label):
            t_in = keep.tile([P, count, TOKENS], BF16, name="%s%d" % (label, first))
            nc.sync.dma_start(out=t_in[:], in_=view[:, first:first + count, :])
            for h in range(count):
                dst[first + h] = t_in[:, h, :]

        w_raw = [keep.tile([P, PACK, D_OUT], BF16, name="wraw%d" % r) for r in range(PARTS)]
        bias_bc = keep.tile([P, D_OUT], BF16, name="bias_bc")
        for h in range(2):
            load(k_sb, k_view, h, 1, "k")
            load(q_sb, q_view, h, 1, "q")
            cols = slice(h * N_MX, (h + 1) * N_MX)
            nc.sync.dma_start(out=w_raw[0][:, :, cols], in_=w_view[:, 0, :, cols])
        load(q_sb, q_view, 2, 2, "q")
        load(k_sb, k_view, 2, 2, "k")
        load(v_sb, v_view, 0, 2, "v")
        nc.sync.dma_start(out=w_raw[1][:], in_=w_view[:, 1])
        load(v_sb, v_view, 2, 2, "v")
        nc.sync.dma_start(out=bias_bc[:], in_=b_out.partition_broadcast(P))
        for first in range(4, HEADS, 2):
            load(q_sb, q_view, first, 2, "q")
            load(k_sb, k_view, first, 2, "k")
            load(v_sb, v_view, first, 2, "v")

        ident = const.tile([P, P], BF16, name="ident")
        masks.make_identity(nc, ident[:])
        ident_f = const.tile([P, P], F32, name="ident_f")
        masks.make_identity(nc, ident_f[:])
        warm = const.tile([P, 2], F32, name="warm")
        nc.vector.memset(warm[:], 0.0)
        nc.scalar.activation(out=warm[:, 1:2], in_=warm[:, 0:1], func=ACT.Exp)

        w_grouped = [keep.tile([P, D_OUT, PACK], BF16, name="wgrp%d" % r, align_bytes=64) for r in range(PARTS)]
        w_codes = keep.tile([P, PARTS, D_OUT], U32, name="w_codes", align_bytes=64)
        w_scales = keep.tile([P, PARTS, D_OUT], U8, name="w_scales", align_bytes=64)

        def regroup_w(engine, piece):
            r, part = divmod(piece, W_PIECES // PARTS)
            cols = slice(part * P, (part + 1) * P)
            engine.tensor_scalar(out=w_grouped[r][:, cols, :],
                                 in0=w_raw[r][:, :, cols].rearrange("p t n -> p n t"),
                                 scalar1=1.0, scalar2=0.0, op0=ALU.mult, op1=ALU.add)

        def quantise_w(r, quarter):
            cols = slice(quarter * D_OUT // 4, (quarter + 1) * D_OUT // 4)
            nc.vector.quantize_mx(out=w_codes[:, r, cols].bitcast(FP8X4), scales=w_scales[:, r, cols],
                                  in_=w_grouped[r][:, cols, :].rearrange("p n t -> p (n t)"))

        qk_ps, qk_t, score, expo, gate_ps, gate_all = {}, {}, {}, {}, {}, {}
        row_max, bias, row_sum, inv_sum, gate = {}, {}, {}, {}, {}

        def transpose_qk(h):
            bank = ps_t.tile([P, 2, TOKENS], BF16, name="tp", tag="tp")
            qk_ps[h] = (bank[:, 0, :], bank[:, 1, :], bank[:])
            if h == 0:
                first = ps_x.tile([P, TOKENS], BF16, name="tp_x", tag="x")
                qk_ps[h] = (bank[:, 0, :], first[:])
            for half, src in ((1, k_sb[h]), (0, q_sb[h])):
                for c in range(CHUNKS):
                    nc.tensor.transpose(out=qk_ps[h][half][:, c * P:(c + 1) * P],
                                        in_=src[:, c * P:(c + 1) * P], identity=ident[:])

        def copy_qk(h):
            qk_t[h] = qk_pool.tile([P, 2, TOKENS], BF16, name="qkT")
            if h == 0:
                nc.vector.tensor_copy(out=qk_t[h][:, 1, :], in_=qk_ps[h][1])
                nc.scalar.copy(out=qk_t[h][:, 0, :], in_=qk_ps[h][0])
            else:
                nc.scalar.copy(out=qk_t[h][:].rearrange("p s n -> p (s n)").bitcast(F32),
                               in_=qk_ps[h][2].rearrange("p s n -> p (s n)").bitcast(F32))

        def scores(s):
            h, c = divmod(s, CHUNKS)
            score[s] = ps_s.tile([P, TOKENS], F32, name="s_ps", tag="s")
            nc.tensor.matmul(out=score[s][:], lhsT=qk_t[h][:, 0, c * P:(c + 1) * P], rhs=qk_t[h][:, 1, :],
                             start=True, stop=True)

        def maximum(s):
            h, c = divmod(s, CHUNKS)
            if c == 0:
                row_max[h] = st_pool.tile([P, CHUNKS], F32, name="mx")
            nc.vector.tensor_reduce(out=row_max[h][:, c:c + 1], in_=score[s][:], axis=AX.X, op=ALU.max)

        def exp_bias(s):
            h, c = divmod(s, CHUNKS)
            if c == 0:
                bias[h] = st_pool.tile([P, CHUNKS], F32, name="nb")
            nc.scalar.mul(out=bias[h][:, c:c + 1], in_=row_max[h][:, c:c + 1], mul=-SCALE)

        def exponentials(s):
            h, c = divmod(s, CHUNKS)
            if c == 0:
                row_sum[h] = st_pool.tile([P, CHUNKS], F32, name="rs")
                expo[h] = e_pool.tile([P, CHUNKS, TOKENS], F32, name="e_t")
            nc.scalar.activation(out=expo[h][:, c, :], in_=score[s][:], func=ACT.Exp,
                                 bias=bias[h][:, c:c + 1], scale=SCALE, accum_out=row_sum[h][:, c:c + 1])

        def reciprocals(h, first, end):
            if first == 0:
                inv_sum[h] = st_pool.tile([P, CHUNKS], F32, name="rr")
            nc.vector.reciprocal(out=inv_sum[h][:, first:end], in_=row_sum[h][:, first:end])

        def rescale_gpsimd(h, c):
            nc.gpsimd.tensor_scalar(out=expo[h][:, c, :], in0=expo[h][:, c, :], scalar1=inv_sum[h][:, c:c + 1],
                                    scalar2=0.0, op0=ALU.mult, op1=ALU.add)

        def rescale_vector(h, c):
            nc.vector.tensor_scalar(out=expo[h][:, c, :], in0=expo[h][:, c, :], scalar1=inv_sum[h][:, c:c + 1],
                                    scalar2=None, op0=ALU.mult)

        def rescale_scalar(h, c):
            nc.scalar.activation(out=expo[h][:, c, :], in_=expo[h][:, c, :], func=ACT.Copy,
                                 scale=inv_sum[h][:, c:c + 1])

        def gate_add(h, j, c, i):
            block = expo[h][:, c, j * P:(j + 1) * P]
            if c == CHUNKS - 1 and h < MV_END:
                nc.tensor.matmul(out=gate_ps[h, j][:, 0:1], lhsT=block, rhs=inv_sum[h][:, c:c + 1],
                                 start=(i == 0), stop=(i == CHUNKS - 1))
            else:
                nc.tensor.matmul(out=gate_ps[h, j], lhsT=block, rhs=ident_f[:],
                                 start=(i == 0), stop=(i == CHUNKS - 1), is_transpose=True)

        def gate_sum(h, j, pool=ps_c, tag="c"):
            if j == 0:
                bank = pool.tile([P, CHUNKS, P], F32, name="cg_" + tag, tag=tag)
                gate_all[h] = bank[:]
            gate_ps[h, j] = gate_all[h][:, j, :]
            for c in range(CHUNKS):
                gate_add(h, j, c, c)

        def reduce_gate(h):
            gate[h] = st_pool.tile([P, CHUNKS], F32, name="cv")
            nc.vector.tensor_reduce(out=gate[h][:], in_=gate_all[h], axis=AX.X, op=ALU.add)

        weighed, a_ps, a_grouped, a_codes, a_scales = {}, {}, {}, {}, {}

        def weigh_gpsimd(h, j):
            g, t = divmod(h, PACK)
            if t == 0 and j == 0:
                weighed[g] = a_pool.tile([P, CHUNKS, 2, P, 2], BF16, name="a4")
            nc.gpsimd.tensor_scalar(out=weighed[g][:, j, :, t * P // PACK:(t + 1) * P // PACK, :],
                                    in0=v_sb[h][:, j * P:(j + 1) * P].rearrange("p (i u e) -> p u i e", u=2, e=2),
                                    scalar1=gate[h][:, j:j + 1], scalar2=0.0, op0=ALU.mult, op1=ALU.add)

        def weigh(h, j):
            g, t = divmod(h, PACK)
            if t == 0 and j == 0:
                weighed[g] = a_pool.tile([P, CHUNKS, 2, P, 2], BF16, name="a4")
            nc.vector.tensor_scalar(out=weighed[g][:, j, :, t * P // PACK:(t + 1) * P // PACK, :],
                                    in0=v_sb[h][:, j * P:(j + 1) * P].rearrange("p (i u e) -> p u i e", u=2, e=2),
                                    scalar1=gate[h][:, j:j + 1], scalar2=None, op0=ALU.mult)

        def transpose_a(g, chunks, pool, tag):
            words = weighed[g][:].rearrange("p j u w e -> p (j u w e)").bitcast(F32)
            bank = pool.tile([P, len(chunks), 2, P], F32, name="ta_" + tag, tag=tag)
            for i, j in enumerate(chunks):
                a_ps[g, j] = bank[:, i]
                for u in range(2):
                    first = (2 * j + u) * P
                    nc.tensor.transpose(out=a_ps[g, j][:, u, :], in_=words[:, first:first + P], identity=ident_f[:])

        def copy_a(copy, g, j):
            if j == 0:
                a_grouped[g] = a_pool.tile([P, CHUNKS, P, PACK], BF16, name="grp", align_bytes=64)
            cols = slice(j * 2 * P, (j + 1) * 2 * P)
            copy(out=a_grouped[g][:].rearrange("p j x t -> p (j x t)").bitcast(F32)[:, cols],
                 in_=a_ps[g, j].rearrange("p u x -> p x u"))

        def quantise_a(g, first, count):
            if first == 0:
                a_codes[g] = keep.tile([P, TOKENS], U32, name="a_codes%d" % g, align_bytes=64)
                a_scales[g] = keep.tile([P, TOKENS], U8, name="a_scales%d" % g, align_bytes=64)
            cols = slice(first * P, (first + count) * P)
            nc.vector.quantize_mx(out=a_codes[g][:, cols].bitcast(FP8X4), scales=a_scales[g][:, cols],
                                  in_=a_grouped[g][:, first:first + count].rearrange("p j x t -> p (j x t)"))

        out_view = out.rearrange("b (p j) n -> b j p n", j=CHUNKS)

        def mx_pass(acc, b, tile, r):
            j, half = divmod(tile, HALVES)
            g = PARTS * b + r
            cols = slice(half * N_MX, (half + 1) * N_MX)
            nc.tensor.matmul_mx(out=acc[:],
                                lhsT=a_codes[g][:, j * P:(j + 1) * P].bitcast(FP8X4),
                                lhsT_scale=a_scales[g][:, j * P:(j + 1) * P],
                                rhs=w_codes[:, r, cols].bitcast(FP8X4), rhs_scale=w_scales[:, r, cols],
                                start=(r == 0), stop=(r == PARTS - 1))

        def emit(acc, b, tile, shared):
            j, half = divmod(tile, HALVES)
            cols = slice(half * N_MX, (half + 1) * N_MX)
            o_sb = o_pool.tile([P, N_MX], F32, name="o_sb")
            if shared:
                nc.scalar.copy(out=o_sb[:], in_=acc[:])
                nc.gpsimd.tensor_tensor(out=o_sb[:], in0=o_sb[:], in1=bias_bc[:, cols], op=ALU.add)
            else:
                nc.vector.tensor_tensor(out=o_sb[:], in0=acc[:], in1=bias_bc[:, cols], op=ALU.add)
            nc.sync.dma_start(out=out_view[b, j][:, cols], in_=o_sb[:])

        def head_in(s, stage):
            h, rest = divmod(s - stage, CHUNKS)
            return h if rest == 0 and 0 <= h < HEADS else -1

        def group_in(s, stage):
            g, rest = divmod(s - (CHUNKS * (PACK - 1) + WEIGH) - stage, CHUNKS * PACK)
            return g if rest == 0 and 0 <= g < GROUPS else -1

        last = HEADS - 1
        acc = {}
        for piece in range(W_EARLY):
            regroup_w(nc.gpsimd, piece)
        for s in range(TRANSPOSE_QK, ALL_CHUNKS):
            if 0 <= s + LEAD < ALL_CHUNKS:
                scores(s + LEAD)
            if head_in(s, TRANSPOSE_QK) >= 0:
                transpose_qk(head_in(s, TRANSPOSE_QK))
            for j in range(CHUNKS):
                if 0 <= head_in(s, GATE[j]) < last - 2:
                    gate_sum(head_in(s, GATE[j]), j)
            if 0 <= group_in(s, TRANSPOSE_A) < GROUPS - 2:
                for pair in range(2):
                    transpose_a(group_in(s, TRANSPOSE_A), (2 * pair, 2 * pair + 1), ps_x, "x")
            for tile in range(TILES):
                if group_in(s, PROJECT[tile]) == PARTS - 1:
                    acc[tile] = ps_x.tile([P, N_MX], F32, name="o_x", tag="x")
                    for r in range(PARTS):
                        mx_pass(acc[tile], 0, tile, r)
            if s >= ALL_CHUNKS - 2:
                for j in (2 * (s - ALL_CHUNKS) + 4, 2 * (s - ALL_CHUNKS) + 5):
                    gate_sum(last - 2, j, ps_t, "tp")
            if 0 <= head_in(s, RECIPROCAL) < last:
                reciprocals(head_in(s, RECIPROCAL), 0, CHUNKS)
            if 0 <= s < ALL_CHUNKS:
                maximum(s)
            if 0 <= head_in(s, REDUCE) < last - 2:
                reduce_gate(head_in(s, REDUCE))
            if 0 <= head_in(s, WEIGH) < last - 2:
                for j in range(CHUNKS):
                    weigh(head_in(s, WEIGH), j)
            if MV_END <= head_in(s, RESCALE_VECTOR) < last - 1:
                rescale_vector(head_in(s, RESCALE_VECTOR), 3)
            if 0 <= group_in(s, QUANTISE_A) < GROUPS - 2:
                for pair in range(2):
                    quantise_a(group_in(s, QUANTISE_A), 2 * pair, 2)
            if 0 <= head_in(s, RECIPROCAL + 1) - W_QUANTISE < 8:
                quantise_w(*divmod(head_in(s, RECIPROCAL + 1) - W_QUANTISE, 4))
            for tile in range(TILES):
                if group_in(s, PROJECT[tile] + 1) == PARTS - 1:
                    emit(acc[tile], 0, tile, False)
            if 0 <= s < ALL_CHUNKS:
                exp_bias(s)
            if 0 <= s - 1:
                exponentials(s - 1)
            if head_in(s, COPY_QK) >= 0:
                copy_qk(head_in(s, COPY_QK))
            for j in range(CHUNKS):
                if 0 <= group_in(s, COPY_A[j]) < GROUPS - 2:
                    copy_a(nc.scalar.copy, group_in(s, COPY_A[j]), j)
            if 0 <= head_in(s, RECIPROCAL) < last:
                for c in range(3 if head_in(s, RECIPROCAL) < last - 1 else 2):
                    rescale_gpsimd(head_in(s, RECIPROCAL), c)
                if W_EARLY + head_in(s, RECIPROCAL) < W_PIECES:
                    regroup_w(nc.gpsimd, W_EARLY + head_in(s, RECIPROCAL))

        def gate_banks(h, banks):
            for j, (pool, tag) in enumerate(banks):
                bank = pool.tile([P, P], F32, name="end_%d_%d" % (h, j), tag=tag)
                gate_ps[h, j] = bank[:]

        junk = const.tile([P, CHUNKS, P], BF16, name="junk")

        def reduce_chunk(engine, h, j):
            if j == 0:
                gate[h] = st_pool.tile([P, CHUNKS], F32, name="cv")
            if engine is nc.scalar:
                nc.scalar.activation(out=junk[:, j, :], in_=gate_ps[h, j], func=ACT.Copy, accum_out=gate[h][:, j:j + 1])
            else:
                nc.vector.tensor_reduce(out=gate[h][:, j:j + 1], in_=gate_ps[h, j], axis=AX.X, op=ALU.add)

        exponentials(ALL_CHUNKS - 1)
        for pair in range(2):
            transpose_a(GROUPS - 2, (2 * pair, 2 * pair + 1), ps_x, "x")
        rescale_vector(last - 1, 2)
        rescale_vector(last - 1, 3)
        reciprocals(last, 0, 2)
        rescale_vector(last, 0)
        rescale_vector(last, 1)
        for j in range(CHUNKS):
            weigh_gpsimd(last - 3, j)
        reciprocals(last, 2, 3)
        rescale_vector(last, 2)
        reciprocals(last, 3, 4)
        rescale_vector(last, 3)
        for j in range(CHUNKS):
            gate_sum(last - 1, j)
        gate_banks(last, ((ps_s, "s"), (ps_s, "s"), (ps_s, "s"), (ps_s, "s")))
        for c in range(CHUNKS):
            for j in range(CHUNKS):
                gate_add(last, j, c, c)
        for j in range(CHUNKS):
            copy_a(nc.scalar.copy, GROUPS - 2, j)
        for h in (last - 2, last - 1):
            for j in range(CHUNKS):
                reduce_chunk(nc.scalar, h, j)
        for j in range(0, CHUNKS, 2):
            quantise_a(GROUPS - 2, j, 2)
        for j in range(CHUNKS):
            weigh_gpsimd(last - 2, j)
        banks = ((ps_x, "x"), (ps_x, "x"), (ps_t, "tp"), (ps_c, "c"))
        for tile, (pool, tag) in enumerate(banks[:2]):
            acc[tile] = pool.tile([P, N_MX], F32, name="o_e%d" % tile, tag=tag)
            mx_pass(acc[tile], 1, tile, 0)
        for j in range(CHUNKS + 1):
            if j < CHUNKS:
                reduce_chunk(nc.vector, last, j)
            if j > 0:
                for h in (last - 1, last):
                    weigh(h, j - 1)
                transpose_a(GROUPS - 1, (j - 1,), ps_s, "s")
                copy_a(nc.scalar.copy, GROUPS - 1, j - 1)
        quantise_a(GROUPS - 1, 0, 1)
        quantise_a(GROUPS - 1, 1, 1)
        for tile in range(TILES):
            if tile >= 2:
                acc[tile] = ps_s.tile([P, N_MX], F32, name="o_s", tag="s")
                mx_pass(acc[tile], 1, tile, 0)
            if tile in (1, 3):
                quantise_a(GROUPS - 1, tile // 2 + 2, 1)
            mx_pass(acc[tile], 1, tile, 1)
            emit(acc[tile], 1, tile, False)
